import numpy as np
import ml_dtypes


def mxq(x, axis, fmt="e4m3"):
    dtype, down = {"e4m3": (ml_dtypes.float8_e4m3fn, 7), "e5m2": (ml_dtypes.float8_e5m2, 14)}[fmt]
    v = np.moveaxis(np.asarray(x, np.float32).astype(ml_dtypes.bfloat16).astype(np.float64), axis, -1)
    blocks = v.reshape(v.shape[:-1] + (-1, 32))
    amax = np.abs(blocks).max(-1, keepdims=True)
    byte = np.maximum(np.where(amax > 0, np.frexp(amax)[1] - 1 + 127, 0) - down, 1)
    scale = np.exp2(byte - 127.0)
    codes = (blocks / scale).astype(np.float32).astype(dtype).astype(np.float64)
    return np.moveaxis((codes * scale).reshape(v.shape), -1, axis)


WIDE = False


def mx_kscale(k):
    if not WIDE:
        return np.ones(k)
    levels = np.array([10, -10, 5, -5, 0])
    a = np.random.permutation(np.resize(levels, k // 512 * 4)).reshape(k // 512, 4)
    idx = np.arange(k)
    return np.exp2(a[idx // 512, idx % 128 // 32])


BF16 = ml_dtypes.bfloat16


def bf(x):
    return np.asarray(x, np.float32).astype(BF16)


def f64(x):
    return np.asarray(x).astype(np.float64)


B, C, H, W = 4, 1024, 32, 32
INTER = C // 2
HW = H * W
HW2 = HW // 2
SP = np.sqrt(2.0 / np.sqrt(C))


def setup_inputs():
    s = mx_kscale(C)
    t = mx_kscale(INTER)
    return {"q": bf(np.random.standard_normal((B, C, H, W)) * s[None, :, None, None]),
            "k": bf(np.random.standard_normal((B, C, H, W)) * s[None, :, None, None]),
            "W_phi": bf(np.random.standard_normal((INTER, C)) * SP / np.sqrt(C) * t[:, None] / s[None, :]),
            "W_theta": bf(np.random.standard_normal((INTER, C)) * SP / np.sqrt(C) / t[:, None] / s[None, :])}


def reference(q, k, W_phi, W_theta):
    qf = f64(q).reshape(B, C, HW)
    kf = f64(k).reshape(B, C, HW)
    phi = (mxq(f64(W_phi), 1, "e4m3") @ mxq(qf, 1, "e4m3")).reshape(B, C, HW2)
    theta = (mxq(f64(W_theta), 1, "e4m3") @ mxq(kf, 1, "e4m3")).reshape(B, C, HW2)
    return mxq(theta, 1, "e4m3").transpose(0, 2, 1) @ mxq(phi, 1, "e4m3")

@@ -1,0 +1,265 @@
+from contextlib import ExitStack
+
+import concourse.mybir as mybir
+from concourse.masks import make_identity
+
+BF16 = mybir.dt.bfloat16
+F32 = mybir.dt.float32
+U32 = mybir.dt.uint32
+U8 = mybir.dt.uint8
+FP8X4 = mybir.dt.float8_e4m3fn_x4
+
+BATCH = 4
+CHANNELS = 1024
+PIXELS = 1024
+INTER = 512
+HALF = PIXELS // 2
+
+P = 128
+PACK = 4
+K_PASS = P * PACK
+CHANNEL_PASSES = CHANNELS // K_PASS
+FOLD_PASSES = 2 * INTER // K_PASS
+PAIR = 2
+BLOCK = 128
+BLOCKS = HALF // BLOCK
+RUN = 4
+
+UNITS = 2 * BATCH
+THETA_UNIT = 1
+LOADS_AHEAD = 4
+
+FLOPS = 2 * BATCH * (2 * INTER * CHANNELS * PIXELS + HALF * HALF * 2 * INTER)
+
+
+def tile_nonlocalblock_pa_t_kernel(tc, q, k, W_phi, W_theta, out):
+    nc = tc.nc
+    maps = (q.rearrange("b c h w -> b c (h w)"), k.rearrange("b c h w -> b c (h w)"))
+    weights = (W_phi, W_theta)
+
+    with ExitStack() as ctx:
+        const_pool = ctx.enter_context(tc.tile_pool(name="const", bufs=1))
+        w_rows_pool = ctx.enter_context(tc.tile_pool(name="w_rows", bufs=2 * FOLD_PASSES))
+        w_grouped_pool = ctx.enter_context(tc.tile_pool(name="w_grouped", bufs=2))
+        raw_pool = ctx.enter_context(tc.tile_pool(name="raw", bufs=LOADS_AHEAD * CHANNEL_PASSES))
+        grouped_pool = ctx.enter_context(tc.tile_pool(name="grouped", bufs=4))
+        x_pool = ctx.enter_context(tc.tile_pool(name="x", bufs=3))
+        folded_pool = ctx.enter_context(tc.tile_pool(name="folded", bufs=4))
+        f_pool = ctx.enter_context(tc.tile_pool(name="f", bufs=4))
+        result_pool = ctx.enter_context(tc.tile_pool(name="result", bufs=6))
+        bank_pool = ctx.enter_context(tc.psum_pool(name="bank", bufs=4))
+        acc_pool = ctx.enter_context(tc.psum_pool(name="acc", bufs=HALF // P))
+        ctx.enter_context(tc.manual_schedule())
+
+        identity = const_pool.tile([P, P], F32)
+        make_identity(nc, identity[:])
+
+        w_codes = []
+        w_scales = []
+        for tensor in range(len(weights)):
+            codes = const_pool.tile(
+                [P, FOLD_PASSES, CHANNEL_PASSES, PAIR, P], U32, name="w_codes_%d" % tensor, align_bytes=64
+            )
+            scales = const_pool.tile(
+                [P, FOLD_PASSES, CHANNEL_PASSES, PAIR, P], U8, name="w_scales_%d" % tensor, align_bytes=64
+            )
+            w_codes.append(codes)
+            w_scales.append(scales)
+
+        w_rows_tiles = {}
+        raw_tiles = {}
+        grouped_tiles = {}
+        x_codes = {}
+        x_scales = {}
+        folded_tiles = {}
+        f_codes = {}
+        f_scales = {}
+
+        def load_weights(tensor, g):
+            w_rows = w_rows_pool.tile([P, PAIR, CHANNELS], BF16)
+            rows = weights[tensor][g * PAIR * P : (g + 1) * PAIR * P, :]
+            nc.sync.dma_start(out=w_rows[:], in_=rows.rearrange("(m e) c -> m e c", e=PAIR))
+            w_rows_tiles[(tensor, g)] = w_rows
+
+        def pack_weights(tensor, g):
+            w_rows = w_rows_tiles[(tensor, g)]
+            words = (
+                w_rows[:]
+                .rearrange("m e c -> m (e c)")
+                .bitcast(F32)
+                .rearrange("m (e cp p u) -> m e cp p u", e=PAIR, cp=CHANNEL_PASSES, u=2)
+            )
+            w_grouped = w_grouped_pool.tile([P, CHANNEL_PASSES, PAIR * P, PACK], BF16, align_bytes=64)
+            for cp in range(CHANNEL_PASSES):
+                flipped = bank_pool.tile([P, 2, PAIR, P], F32, tag="bank")
+                for u in range(2):
+                    for e in range(PAIR):
+                        nc.tensor.transpose(flipped[:, u, e, :], words[:, e, cp, :, u], identity[:])
+                nc.scalar.copy(
+                    out=w_grouped[:, cp, :, :]
+                    .rearrange("p x t -> p (x t)")
+                    .bitcast(F32)
+                    .rearrange("p (x u) -> p x u", u=2),
+                    in_=flipped[:].rearrange("p u e m -> p (e m) u"),
+                )
+            nc.vector.quantize_mx(
+                out=w_codes[tensor][:, g, :, :, :].rearrange("p cp e m -> p (cp e m)").bitcast(FP8X4),
+                scales=w_scales[tensor][:, g, :, :, :].rearrange("p cp e m -> p (cp e m)"),
+                in_=w_grouped[:].rearrange("p cp x t -> p (cp x t)"),
+            )
+
+        def load_chunk(u, cp):
+            batch, tensor = divmod(u, 2)
+            raw = raw_pool.tile([P, PACK, PIXELS], BF16)
+            rows = maps[tensor][batch, cp * K_PASS : (cp + 1) * K_PASS, :]
+            nc.sync.dma_start(out=raw[:], in_=rows.rearrange("(p t) w -> p t w", t=PACK))
+            raw_tiles[(u, cp)] = raw
+
+        def scalar_regroups(cp, j):
+            return cp == CHANNEL_PASSES - 1 and j == PAIR - 1
+
+        def regroup(u, cp, j):
+            raw = raw_tiles[(u, cp)]
+            if j == 0:
+                grouped = grouped_pool.tile([P, BLOCKS, PAIR, BLOCK, PACK], BF16, align_bytes=64)
+                grouped_tiles[(u, cp)] = grouped
+            grouped = grouped_tiles[(u, cp)]
+            half = raw[:, :, j * HALF : (j + 1) * HALF]
+            if scalar_regroups(cp, j):
+                for block in range(BLOCKS):
+                    nc.scalar.copy(
+                        out=grouped[:, block, j, :, :].rearrange("p (c i) t -> p c t i", i=RUN),
+                        in_=half[:, :, block * BLOCK : (block + 1) * BLOCK].rearrange(
+                            "p t (c i) -> p c t i", i=RUN
+                        ),
+                    )
+            else:
+                nc.vector.tensor_copy(
+                    out=grouped[:, :, j, :, :].rearrange("p b (c i) t -> p b c t i", i=RUN),
+                    in_=half.rearrange("p t (b c i) -> p b c t i", b=BLOCKS, i=RUN),
+                )
+
+        def quantise(u, cp):
+            if cp == 0:
+                codes = x_pool.tile([P, CHANNEL_PASSES, PIXELS], U32, align_bytes=64)
+                scales = x_pool.tile([P, CHANNEL_PASSES, PIXELS], U8, align_bytes=64)
+                x_codes[u] = codes
+                x_scales[u] = scales
+            grouped = grouped_tiles[(u, cp)]
+            nc.vector.quantize_mx(
+                out=x_codes[u][:, cp, :].bitcast(FP8X4),
+                scales=x_scales[u][:, cp, :],
+                in_=grouped[:].rearrange("p b j r t -> p (b j r t)"),
+            )
+
+        def project(u, g):
+            tensor = u % 2
+            folded = folded_pool.tile([P, HALF, PACK], BF16, align_bytes=64)
+            for block in range(BLOCKS):
+                columns = slice(block * PAIR * BLOCK, (block + 1) * PAIR * BLOCK)
+                bank = bank_pool.tile([P, PAIR, PAIR, BLOCK], F32, tag="bank")
+                for e in range(PAIR):
+                    for cp in range(CHANNEL_PASSES):
+                        nc.tensor.matmul_mx(
+                            out=bank[:, e, :, :].rearrange("m j r -> m (j r)"),
+                            lhsT=w_codes[tensor][:, g, cp, e, :].bitcast(FP8X4),
+                            lhsT_scale=w_scales[tensor][:, g, cp, e, :],
+                            rhs=x_codes[u][:, cp, columns].bitcast(FP8X4),
+                            rhs_scale=x_scales[u][:, cp, columns],
+                            start=(cp == 0),
+                            stop=(cp == CHANNEL_PASSES - 1),
+                        )
+                nc.scalar.copy(
+                    out=folded[:, block * BLOCK : (block + 1) * BLOCK, :],
+                    in_=bank[:].rearrange("m e j r -> m r (e j)"),
+                )
+            folded_tiles[(u, g)] = folded
+
+        def quantise_fold(u, g):
+            if g == 0:
+                codes = f_pool.tile([P, FOLD_PASSES, HALF], U32, align_bytes=64)
+                scales = f_pool.tile([P, FOLD_PASSES, HALF], U8, align_bytes=64)
+                f_codes[u] = codes
+                f_scales[u] = scales
+            folded = folded_tiles[(u, g)]
+            nc.vector.quantize_mx(
+                out=f_codes[u][:, g, :].bitcast(FP8X4),
+                scales=f_scales[u][:, g, :],
+                in_=folded[:].rearrange("m n t -> m (n t)"),
+            )
+
+        def affinity(batch):
+            phi, theta = 2 * batch, 2 * batch + 1
+            accs = []
+            for i in range(HALF // P):
+                acc = acc_pool.tile([P, HALF], F32)
+                accs.append(acc)
+            for g in range(FOLD_PASSES):
+                for i in range(HALF // P):
+                    nc.tensor.matmul_mx(
+                        out=accs[i][:],
+                        lhsT=f_codes[theta][:, g, i * P : (i + 1) * P].bitcast(FP8X4),
+                        lhsT_scale=f_scales[theta][:, g, i * P : (i + 1) * P],
+                        rhs=f_codes[phi][:, g, :].bitcast(FP8X4),
+                        rhs_scale=f_scales[phi][:, g, :],
+                        start=(g == 0),
+                        stop=(g == FOLD_PASSES - 1),
+                    )
+            for i in range(HALF // P):
+                result = result_pool.tile([P, HALF], F32)
+                if i % 2 == 0:
+                    nc.scalar.copy(out=result[:], in_=accs[i][:])
+                else:
+                    nc.vector.tensor_copy(out=result[:], in_=accs[i][:])
+                nc.sync.dma_start(out=out[batch, i * P : (i + 1) * P, :], in_=result[:])
+
+        load_chunk(0, 0)
+        load_weights(0, 0)
+        load_chunk(0, 1)
+        load_weights(0, 1)
+        load_weights(1, 0)
+        load_chunk(1, 0)
+        load_chunk(1, 1)
+        load_weights(1, 1)
+        for u in range(2, LOADS_AHEAD):
+            for cp in range(CHANNEL_PASSES):
+                load_chunk(u, cp)
+
+        regroup(0, 0, 0)
+        regroup(0, 0, 1)
+        quantise(0, 0)
+        pack_weights(0, 0)
+        regroup(0, 1, 0)
+        regroup(0, 1, 1)
+        quantise(0, 1)
+        pack_weights(0, 1)
+
+        pieces = [(cp, j) for cp in range(CHANNEL_PASSES) for j in range(PAIR)]
+        for s in range(UNITS + 1):
+            ahead = s + 1
+            if s + LOADS_AHEAD < UNITS:
+                for cp in range(CHANNEL_PASSES):
+                    load_chunk(s + LOADS_AHEAD, cp)
+            if ahead < UNITS:
+                for cp, j in pieces:
+                    if not scalar_regroups(cp, j):
+                        regroup(ahead, cp, j)
+            if s >= 1:
+                quantise_fold(s - 1, 1)
+            if s < UNITS:
+                project(s, 0)
+            if ahead == THETA_UNIT:
+                pack_weights(1, 0)
+            if ahead < UNITS:
+                for cp, j in pieces:
+                    if scalar_regroups(cp, j):
+                        regroup(ahead, cp, j)
+                for cp in range(CHANNEL_PASSES):
+                    quantise(ahead, cp)
+            if s < UNITS:
+                project(s, 1)
+                quantise_fold(s, 0)
+            if ahead == THETA_UNIT:
+                pack_weights(1, 1)
+            if s >= 2 and s % 2 == 0:
+                affinity(s // 2 - 1)

@@ -26,7 +26,7 @@ BLOCKS = HALF // BLOCK
 RUN = 4
 
 UNITS = 2 * BATCH
-THETA_UNIT = 1
+LEAD = 1
 LOADS_AHEAD = 4
 
 FLOPS = 2 * BATCH * (2 * INTER * CHANNELS * PIXELS + HALF * HALF * 2 * INTER)
@@ -49,7 +49,6 @@ def tile_nonlocalblock_pa_t_kernel(tc, q, k, W_phi, W_theta, out):
         result_pool = ctx.enter_context(tc.tile_pool(name="result", bufs=6))
         bank_pool = ctx.enter_context(tc.psum_pool(name="bank", bufs=4))
         acc_pool = ctx.enter_context(tc.psum_pool(name="acc", bufs=HALF // P))
-        ctx.enter_context(tc.manual_schedule())
 
         identity = const_pool.tile([P, P], F32)
         make_identity(nc, identity[:])
@@ -225,41 +224,25 @@ def tile_nonlocalblock_pa_t_kernel(tc, q, k, W_phi, W_theta, out):
             for cp in range(CHANNEL_PASSES):
                 load_chunk(u, cp)
 
-        regroup(0, 0, 0)
-        regroup(0, 0, 1)
-        quantise(0, 0)
-        pack_weights(0, 0)
-        regroup(0, 1, 0)
-        regroup(0, 1, 1)
-        quantise(0, 1)
-        pack_weights(0, 1)
+        def prepare(u):
+            for cp in range(CHANNEL_PASSES):
+                for j in range(PAIR):
+                    regroup(u, cp, j)
+                quantise(u, cp)
 
-        pieces = [(cp, j) for cp in range(CHANNEL_PASSES) for j in range(PAIR)]
-        for s in range(UNITS + 1):
-            ahead = s + 1
-            if s + LOADS_AHEAD < UNITS:
+        for tensor in range(len(weights)):
+            for g in range(FOLD_PASSES):
+                pack_weights(tensor, g)
+        for u in range(LEAD):
+            prepare(u)
+        for u in range(UNITS):
+            if u + LOADS_AHEAD < UNITS:
                 for cp in range(CHANNEL_PASSES):
-                    load_chunk(s + LOADS_AHEAD, cp)
-            if ahead < UNITS:
-                for cp, j in pieces:
-                    if not scalar_regroups(cp, j):
-                        regroup(ahead, cp, j)
-            if s >= 1:
-                quantise_fold(s - 1, 1)
-            if s < UNITS:
-                project(s, 0)
-            if ahead == THETA_UNIT:
-                pack_weights(1, 0)
-            if ahead < UNITS:
-                for cp, j in pieces:
-                    if scalar_regroups(cp, j):
-                        regroup(ahead, cp, j)
-                for cp in range(CHANNEL_PASSES):
-                    quantise(ahead, cp)
-            if s < UNITS:
-                project(s, 1)
-                quantise_fold(s, 0)
-            if ahead == THETA_UNIT:
-                pack_weights(1, 1)
-            if s >= 2 and s % 2 == 0:
-                affinity(s // 2 - 1)
+                    load_chunk(u + LOADS_AHEAD, cp)
+            if u + LEAD < UNITS:
+                prepare(u + LEAD)
+            for g in range(FOLD_PASSES):
+                project(u, g)
+                quantise_fold(u, g)
+            if u % 2 == 1:
+                affinity(u // 2)

@@ -23,10 +23,11 @@ FOLD_PASSES = 2 * INTER // K_PASS
 PAIR = 2
 BLOCK = 128
 BLOCKS = HALF // BLOCK
+SCALAR_BLOCKS = 3
 RUN = 4
 
 UNITS = 2 * BATCH
-LEAD = 1
+LEAD = 2
 LOADS_AHEAD = 4
 
 FLOPS = 2 * BATCH * (2 * INTER * CHANNELS * PIXELS + HALF * HALF * 2 * INTER)
@@ -43,8 +44,8 @@ def tile_nonlocalblock_pa_t_kernel(tc, q, k, W_phi, W_theta, out):
         w_grouped_pool = ctx.enter_context(tc.tile_pool(name="w_grouped", bufs=2))
         raw_pool = ctx.enter_context(tc.tile_pool(name="raw", bufs=LOADS_AHEAD * CHANNEL_PASSES))
         grouped_pool = ctx.enter_context(tc.tile_pool(name="grouped", bufs=4))
-        x_pool = ctx.enter_context(tc.tile_pool(name="x", bufs=3))
-        folded_pool = ctx.enter_context(tc.tile_pool(name="folded", bufs=4))
+        x_pool = ctx.enter_context(tc.tile_pool(name="x", bufs=LEAD + 2))
+        folded_pool = ctx.enter_context(tc.tile_pool(name="folded", bufs=6))
         f_pool = ctx.enter_context(tc.tile_pool(name="f", bufs=4))
         result_pool = ctx.enter_context(tc.tile_pool(name="result", bufs=6))
         bank_pool = ctx.enter_context(tc.psum_pool(name="bank", bufs=4))
@@ -114,9 +115,6 @@ def tile_nonlocalblock_pa_t_kernel(tc, q, k, W_phi, W_theta, out):
             nc.sync.dma_start(out=raw[:], in_=rows.rearrange("(p t) w -> p t w", t=PACK))
             raw_tiles[(u, cp)] = raw
 
-        def scalar_regroups(cp, j):
-            return cp == CHANNEL_PASSES - 1 and j == PAIR - 1
-
         def regroup(u, cp, j):
             raw = raw_tiles[(u, cp)]
             if j == 0:
@@ -124,18 +122,18 @@ def tile_nonlocalblock_pa_t_kernel(tc, q, k, W_phi, W_theta, out):
                 grouped_tiles[(u, cp)] = grouped
             grouped = grouped_tiles[(u, cp)]
             half = raw[:, :, j * HALF : (j + 1) * HALF]
-            if scalar_regroups(cp, j):
-                for block in range(BLOCKS):
-                    nc.scalar.copy(
-                        out=grouped[:, block, j, :, :].rearrange("p (c i) t -> p c t i", i=RUN),
-                        in_=half[:, :, block * BLOCK : (block + 1) * BLOCK].rearrange(
-                            "p t (c i) -> p c t i", i=RUN
-                        ),
-                    )
-            else:
-                nc.vector.tensor_copy(
-                    out=grouped[:, :, j, :, :].rearrange("p b (c i) t -> p b c t i", i=RUN),
-                    in_=half.rearrange("p t (b c i) -> p b c t i", b=BLOCKS, i=RUN),
+            last_quarter = cp == CHANNEL_PASSES - 1 and j == PAIR - 1
+            vector_blocks = BLOCKS - SCALAR_BLOCKS if last_quarter else BLOCKS
+            nc.vector.tensor_copy(
+                out=grouped[:, :vector_blocks, j, :, :].rearrange("p b (c i) t -> p b c t i", i=RUN),
+                in_=half[:, :, : vector_blocks * BLOCK].rearrange(
+                    "p t (b c i) -> p b c t i", b=vector_blocks, i=RUN
+                ),
+            )
+            for block in range(vector_blocks, BLOCKS):
+                nc.scalar.copy(
+                    out=grouped[:, block, j, :, :].rearrange("p (c i) t -> p c t i", i=RUN),
+                    in_=half[:, :, block * BLOCK : (block + 1) * BLOCK].rearrange("p t (c i) -> p c t i", i=RUN),
                 )
 
         def quantise(u, cp):
@@ -150,6 +148,12 @@ def tile_nonlocalblock_pa_t_kernel(tc, q, k, W_phi, W_theta, out):
                 scales=x_scales[u][:, cp, :],
                 in_=grouped[:].rearrange("p b j r t -> p (b j r t)"),
             )
+
+        def empty_bank(stage, index, out, in_):
+            if stage >= BATCH and index % 2 == 1:
+                nc.vector.tensor_copy(out=out, in_=in_)
+            else:
+                nc.scalar.copy(out=out, in_=in_)
 
         def project(u, g):
             tensor = u % 2
@@ -168,7 +172,9 @@ def tile_nonlocalblock_pa_t_kernel(tc, q, k, W_phi, W_theta, out):
                             start=(cp == 0),
                             stop=(cp == CHANNEL_PASSES - 1),
                         )
-                nc.scalar.copy(
+                empty_bank(
+                    (u + 1) // 2,
+                    block,
                     out=folded[:, block * BLOCK : (block + 1) * BLOCK, :],
                     in_=bank[:].rearrange("m e j r -> m r (e j)"),
                 )
@@ -206,10 +212,7 @@ def tile_nonlocalblock_pa_t_kernel(tc, q, k, W_phi, W_theta, out):
                     )
             for i in range(HALF // P):
                 result = result_pool.tile([P, HALF], F32)
-                if i % 2 == 0:
-                    nc.scalar.copy(out=result[:], in_=accs[i][:])
-                else:
-                    nc.vector.tensor_copy(out=result[:], in_=accs[i][:])
+                empty_bank(batch + 1, i, out=result[:], in_=accs[i][:])
                 nc.sync.dma_start(out=out[batch, i * P : (i + 1) * P, :], in_=result[:])
 
         load_chunk(0, 0)

@@ -24,7 +24,7 @@ PAIR = 2
 BLOCK = 128
 BLOCKS = HALF // BLOCK
 SCALAR_BLOCKS = 3
-RUN = 4
+RUN = 8
 
 UNITS = 2 * BATCH
 LEAD = 2

@@ -23,10 +23,14 @@ FOLD_PASSES = 2 * INTER // K_PASS
 PAIR = 2
 BLOCK = 128
 BLOCKS = HALF // BLOCK
-SCALAR_BLOCKS = 3
 RUN = 8
+RUNS = HALF // RUN
+BLOCK_RUNS = BLOCK // RUN
+SCALAR_RUNS = 16
+SCALAR_PIECE = 16
 
 UNITS = 2 * BATCH
+LAST_PARTS = 2
 LEAD = 2
 LOADS_AHEAD = 4
 
@@ -45,7 +49,7 @@ def tile_nonlocalblock_pa_t_kernel(tc, q, k, W_phi, W_theta, out):
         raw_pool = ctx.enter_context(tc.tile_pool(name="raw", bufs=LOADS_AHEAD * CHANNEL_PASSES))
         grouped_pool = ctx.enter_context(tc.tile_pool(name="grouped", bufs=4))
         x_pool = ctx.enter_context(tc.tile_pool(name="x", bufs=LEAD + 2))
-        folded_pool = ctx.enter_context(tc.tile_pool(name="folded", bufs=6))
+        folded_pool = ctx.enter_context(tc.tile_pool(name="folded", bufs=3))
         f_pool = ctx.enter_context(tc.tile_pool(name="f", bufs=4))
         result_pool = ctx.enter_context(tc.tile_pool(name="result", bufs=6))
         bank_pool = ctx.enter_context(tc.psum_pool(name="bank", bufs=4))
@@ -115,38 +119,38 @@ def tile_nonlocalblock_pa_t_kernel(tc, q, k, W_phi, W_theta, out):
             nc.sync.dma_start(out=raw[:], in_=rows.rearrange("(p t) w -> p t w", t=PACK))
             raw_tiles[(u, cp)] = raw
 
-        def regroup(u, cp, j):
+        def parts_of(u):
+            return LAST_PARTS if u == UNITS - 1 else 1
+
+        def regroup(u, part, cp):
             raw = raw_tiles[(u, cp)]
-            if j == 0:
-                grouped = grouped_pool.tile([P, BLOCKS, PAIR, BLOCK, PACK], BF16, align_bytes=64)
+            if part == 0:
+                grouped = grouped_pool.tile([P, RUNS, PAIR, RUN, PACK], BF16, align_bytes=64)
                 grouped_tiles[(u, cp)] = grouped
             grouped = grouped_tiles[(u, cp)]
-            half = raw[:, :, j * HALF : (j + 1) * HALF]
-            last_quarter = cp == CHANNEL_PASSES - 1 and j == PAIR - 1
-            vector_blocks = BLOCKS - SCALAR_BLOCKS if last_quarter else BLOCKS
-            nc.vector.tensor_copy(
-                out=grouped[:, :vector_blocks, j, :, :].rearrange("p b (c i) t -> p b c t i", i=RUN),
-                in_=half[:, :, : vector_blocks * BLOCK].rearrange(
-                    "p t (b c i) -> p b c t i", b=vector_blocks, i=RUN
-                ),
-            )
-            for block in range(vector_blocks, BLOCKS):
-                nc.scalar.copy(
-                    out=grouped[:, block, j, :, :].rearrange("p (c i) t -> p c t i", i=RUN),
-                    in_=half[:, :, block * BLOCK : (block + 1) * BLOCK].rearrange("p t (c i) -> p c t i", i=RUN),
-                )
+            source = raw[:].rearrange("p t (j c i) -> p c j t i", j=PAIR, i=RUN)
+            target = grouped[:].rearrange("p c j i t -> p c j t i")
+            parts = parts_of(u)
+            begin = part * RUNS // parts
+            end = begin + RUNS // parts
+            middle = end - SCALAR_RUNS // parts if cp == CHANNEL_PASSES - 1 else end
+            nc.vector.tensor_copy(out=target[:, begin:middle], in_=source[:, begin:middle])
+            if middle < end:
+                nc.scalar.copy(out=target[:, middle:end], in_=source[:, middle:end])
 
-        def quantise(u, cp):
-            if cp == 0:
+        def quantise(u, part, cp):
+            if part == 0 and cp == 0:
                 codes = x_pool.tile([P, CHANNEL_PASSES, PIXELS], U32, align_bytes=64)
                 scales = x_pool.tile([P, CHANNEL_PASSES, PIXELS], U8, align_bytes=64)
                 x_codes[u] = codes
                 x_scales[u] = scales
-            grouped = grouped_tiles[(u, cp)]
+            parts = parts_of(u)
+            columns = slice(part * PIXELS // parts, (part + 1) * PIXELS // parts)
+            runs = slice(part * RUNS // parts, (part + 1) * RUNS // parts)
             nc.vector.quantize_mx(
-                out=x_codes[u][:, cp, :].bitcast(FP8X4),
-                scales=x_scales[u][:, cp, :],
-                in_=grouped[:].rearrange("p b j r t -> p (b j r t)"),
+                out=x_codes[u][:, cp, columns].bitcast(FP8X4),
+                scales=x_scales[u][:, cp, columns],
+                in_=grouped_tiles[(u, cp)][:, runs].rearrange("p c j i t -> p (c j i t)"),
             )
 
         def empty_bank(stage, index, out, in_):
@@ -155,16 +159,21 @@ def tile_nonlocalblock_pa_t_kernel(tc, q, k, W_phi, W_theta, out):
             else:
                 nc.scalar.copy(out=out, in_=in_)
 
-        def project(u, g):
+        def project(u, part, g):
             tensor = u % 2
-            folded = folded_pool.tile([P, HALF, PACK], BF16, align_bytes=64)
-            for block in range(BLOCKS):
-                columns = slice(block * PAIR * BLOCK, (block + 1) * PAIR * BLOCK)
-                bank = bank_pool.tile([P, PAIR, PAIR, BLOCK], F32, tag="bank")
+            parts = parts_of(u)
+            if part == 0 and g == 0:
+                folded = folded_pool.tile([P, parts, FOLD_PASSES, HALF // parts, PACK], BF16, align_bytes=64)
+                folded_tiles[u] = folded
+            folded = folded_tiles[u]
+            for block in range(BLOCKS // parts):
+                first = (part * BLOCKS // parts + block) * PAIR * BLOCK
+                columns = slice(first, first + PAIR * BLOCK)
+                bank = bank_pool.tile([P, PAIR, BLOCK_RUNS, PAIR, RUN], F32, tag="bank")
                 for e in range(PAIR):
                     for cp in range(CHANNEL_PASSES):
                         nc.tensor.matmul_mx(
-                            out=bank[:, e, :, :].rearrange("m j r -> m (j r)"),
+                            out=bank[:, e, :, :, :].rearrange("m c j i -> m (c j i)"),
                             lhsT=w_codes[tensor][:, g, cp, e, :].bitcast(FP8X4),
                             lhsT_scale=w_scales[tensor][:, g, cp, e, :],
                             rhs=x_codes[u][:, cp, columns].bitcast(FP8X4),
@@ -175,44 +184,43 @@ def tile_nonlocalblock_pa_t_kernel(tc, q, k, W_phi, W_theta, out):
                 empty_bank(
                     (u + 1) // 2,
                     block,
-                    out=folded[:, block * BLOCK : (block + 1) * BLOCK, :],
-                    in_=bank[:].rearrange("m e j r -> m r (e j)"),
+                    out=folded[:, part, g, block * BLOCK : (block + 1) * BLOCK, :].rearrange(
+                        "m (c i) (e j) -> m c i e j", i=RUN, e=PAIR
+                    ),
+                    in_=bank[:].rearrange("m e c j i -> m c i e j"),
                 )
-            folded_tiles[(u, g)] = folded
 
-        def quantise_fold(u, g):
-            if g == 0:
-                codes = f_pool.tile([P, FOLD_PASSES, HALF], U32, align_bytes=64)
-                scales = f_pool.tile([P, FOLD_PASSES, HALF], U8, align_bytes=64)
+        def quantise_fold(u, part):
+            parts = parts_of(u)
+            if part == 0:
+                codes = f_pool.tile([P, parts, FOLD_PASSES, HALF // parts], U32, align_bytes=64)
+                scales = f_pool.tile([P, parts, FOLD_PASSES, HALF // parts], U8, align_bytes=64)
                 f_codes[u] = codes
                 f_scales[u] = scales
-            folded = folded_tiles[(u, g)]
             nc.vector.quantize_mx(
-                out=f_codes[u][:, g, :].bitcast(FP8X4),
-                scales=f_scales[u][:, g, :],
-                in_=folded[:].rearrange("m n t -> m (n t)"),
+                out=f_codes[u][:, part, :, :].rearrange("m g n -> m (g n)").bitcast(FP8X4),
+                scales=f_scales[u][:, part, :, :].rearrange("m g n -> m (g n)"),
+                in_=folded_tiles[u][:, part, :, :, :].rearrange("m g n t -> m (g n t)"),
             )
 
-        def affinity(batch):
+        def affinity(batch, part):
             phi, theta = 2 * batch, 2 * batch + 1
-            accs = []
-            for i in range(HALF // P):
+            parts = parts_of(theta)
+            for tile in range(HALF // P // parts):
                 acc = acc_pool.tile([P, HALF], F32)
-                accs.append(acc)
-            for g in range(FOLD_PASSES):
-                for i in range(HALF // P):
+                for g in range(FOLD_PASSES):
                     nc.tensor.matmul_mx(
-                        out=accs[i][:],
-                        lhsT=f_codes[theta][:, g, i * P : (i + 1) * P].bitcast(FP8X4),
-                        lhsT_scale=f_scales[theta][:, g, i * P : (i + 1) * P],
-                        rhs=f_codes[phi][:, g, :].bitcast(FP8X4),
-                        rhs_scale=f_scales[phi][:, g, :],
+                        out=acc[:],
+                        lhsT=f_codes[theta][:, part, g, tile * P : (tile + 1) * P].bitcast(FP8X4),
+                        lhsT_scale=f_scales[theta][:, part, g, tile * P : (tile + 1) * P],
+                        rhs=f_codes[phi][:, 0, g, :].bitcast(FP8X4),
+                        rhs_scale=f_scales[phi][:, 0, g, :],
                         start=(g == 0),
                         stop=(g == FOLD_PASSES - 1),
                     )
-            for i in range(HALF // P):
+                i = part * (HALF // P // parts) + tile
                 result = result_pool.tile([P, HALF], F32)
-                empty_bank(batch + 1, i, out=result[:], in_=accs[i][:])
+                empty_bank(batch + 1, i, out=result[:], in_=acc[:])
                 nc.sync.dma_start(out=out[batch, i * P : (i + 1) * P, :], in_=result[:])
 
         load_chunk(0, 0)
@@ -228,10 +236,10 @@ def tile_nonlocalblock_pa_t_kernel(tc, q, k, W_phi, W_theta, out):
                 load_chunk(u, cp)
 
         def prepare(u):
-            for cp in range(CHANNEL_PASSES):
-                for j in range(PAIR):
-                    regroup(u, cp, j)
-                quantise(u, cp)
+            for part in range(parts_of(u)):
+                for cp in range(CHANNEL_PASSES):
+                    regroup(u, part, cp)
+                    quantise(u, part, cp)
 
         for tensor in range(len(weights)):
             for g in range(FOLD_PASSES):
@@ -244,8 +252,9 @@ def tile_nonlocalblock_pa_t_kernel(tc, q, k, W_phi, W_theta, out):
                     load_chunk(u + LOADS_AHEAD, cp)
             if u + LEAD < UNITS:
                 prepare(u + LEAD)
-            for g in range(FOLD_PASSES):
-                project(u, g)
-                quantise_fold(u, g)
-            if u % 2 == 1:
-                affinity(u // 2)
+            for part in range(parts_of(u)):
+                for g in range(FOLD_PASSES):
+                    project(u, part, g)
+                quantise_fold(u, part)
+                if u % 2 == 1:
+                    affinity(u // 2, part)

@@ -26,11 +26,10 @@ BLOCKS = HALF // BLOCK
 RUN = 8
 RUNS = HALF // RUN
 BLOCK_RUNS = BLOCK // RUN
-SCALAR_RUNS = 16
-SCALAR_PIECE = 16
+SCALAR_RUNS = 6
 
 UNITS = 2 * BATCH
-LAST_PARTS = 2
+LAST_PARTS = (2, 1, 1)
 LEAD = 2
 LOADS_AHEAD = 4
 
@@ -71,13 +70,16 @@ def tile_nonlocalblock_pa_t_kernel(tc, q, k, W_phi, W_theta, out):
             w_scales.append(scales)
 
         w_rows_tiles = {}
+        w_grouped_tiles = {}
         raw_tiles = {}
+        raw_halves = []
         grouped_tiles = {}
         x_codes = {}
         x_scales = {}
         folded_tiles = {}
         f_codes = {}
         f_scales = {}
+        accs = {}
 
         def load_weights(tensor, g):
             w_rows = w_rows_pool.tile([P, PAIR, CHANNELS], BF16)
@@ -85,7 +87,7 @@ def tile_nonlocalblock_pa_t_kernel(tc, q, k, W_phi, W_theta, out):
             nc.sync.dma_start(out=w_rows[:], in_=rows.rearrange("(m e) c -> m e c", e=PAIR))
             w_rows_tiles[(tensor, g)] = w_rows
 
-        def pack_weights(tensor, g):
+        def transpose_weights(tensor, g):
             w_rows = w_rows_tiles[(tensor, g)]
             words = (
                 w_rows[:]
@@ -106,6 +108,10 @@ def tile_nonlocalblock_pa_t_kernel(tc, q, k, W_phi, W_theta, out):
                     .rearrange("p (x u) -> p x u", u=2),
                     in_=flipped[:].rearrange("p u e m -> p (e m) u"),
                 )
+            w_grouped_tiles[(tensor, g)] = w_grouped
+
+        def quantise_weights(tensor, g):
+            w_grouped = w_grouped_tiles[(tensor, g)]
             nc.vector.quantize_mx(
                 out=w_codes[tensor][:, g, :, :, :].rearrange("p cp e m -> p (cp e m)").bitcast(FP8X4),
                 scales=w_scales[tensor][:, g, :, :, :].rearrange("p cp e m -> p (cp e m)"),
@@ -114,29 +120,44 @@ def tile_nonlocalblock_pa_t_kernel(tc, q, k, W_phi, W_theta, out):
 
         def load_chunk(u, cp):
             batch, tensor = divmod(u, 2)
-            raw = raw_pool.tile([P, PACK, PIXELS], BF16)
-            rows = maps[tensor][batch, cp * K_PASS : (cp + 1) * K_PASS, :]
-            nc.sync.dma_start(out=raw[:], in_=rows.rearrange("(p t) w -> p t w", t=PACK))
-            raw_tiles[(u, cp)] = raw
+            rows = maps[tensor][batch, cp * K_PASS : (cp + 1) * K_PASS, :].rearrange("(p t) w -> p t w", t=PACK)
+            if u == 0 and cp == 0:
+                for j in range(PAIR):
+                    raw_half = const_pool.tile([P, PACK, HALF], BF16, name="raw_half_%d" % j)
+                    nc.sync.dma_start(out=raw_half[:], in_=rows[:, :, j * HALF : (j + 1) * HALF])
+                    raw_halves.append(raw_half)
+            else:
+                raw = raw_pool.tile([P, PACK, PIXELS], BF16)
+                nc.sync.dma_start(out=raw[:], in_=rows)
+                raw_tiles[(u, cp)] = raw
 
         def parts_of(u):
-            return LAST_PARTS if u == UNITS - 1 else 1
+            return LAST_PARTS if u == UNITS - 1 else (BLOCKS,)
 
-        def regroup(u, part, cp):
-            raw = raw_tiles[(u, cp)]
-            if part == 0:
+        def blocks_of(u, part):
+            first = sum(parts_of(u)[:part])
+            return slice(first, first + parts_of(u)[part])
+
+        def regroup(engine, u, part, cp):
+            if (u, cp) not in grouped_tiles:
                 grouped = grouped_pool.tile([P, RUNS, PAIR, RUN, PACK], BF16, align_bytes=64)
                 grouped_tiles[(u, cp)] = grouped
             grouped = grouped_tiles[(u, cp)]
-            source = raw[:].rearrange("p t (j c i) -> p c j t i", j=PAIR, i=RUN)
             target = grouped[:].rearrange("p c j i t -> p c j t i")
-            parts = parts_of(u)
-            begin = part * RUNS // parts
-            end = begin + RUNS // parts
-            middle = end - SCALAR_RUNS // parts if cp == CHANNEL_PASSES - 1 else end
-            nc.vector.tensor_copy(out=target[:, begin:middle], in_=source[:, begin:middle])
-            if middle < end:
+            if u == 0 and cp == 0:
+                for j in range(PAIR):
+                    nc.vector.tensor_copy(
+                        out=target[:, :, j], in_=raw_halves[j][:].rearrange("p t (c i) -> p c t i", i=RUN)
+                    )
+                return
+            source = raw_tiles[(u, cp)][:].rearrange("p t (j c i) -> p c j t i", j=PAIR, i=RUN)
+            blocks = blocks_of(u, part)
+            begin, end = blocks.start * BLOCK_RUNS, blocks.stop * BLOCK_RUNS
+            middle = end - (blocks.stop - blocks.start) * SCALAR_RUNS if cp == CHANNEL_PASSES - 1 else end
+            if engine is nc.scalar:
                 nc.scalar.copy(out=target[:, middle:end], in_=source[:, middle:end])
+            else:
+                nc.vector.tensor_copy(out=target[:, begin:middle], in_=source[:, begin:middle])
 
         def quantise(u, part, cp):
             if part == 0 and cp == 0:
@@ -144,31 +165,24 @@ def tile_nonlocalblock_pa_t_kernel(tc, q, k, W_phi, W_theta, out):
                 scales = x_pool.tile([P, CHANNEL_PASSES, PIXELS], U8, align_bytes=64)
                 x_codes[u] = codes
                 x_scales[u] = scales
-            parts = parts_of(u)
-            columns = slice(part * PIXELS // parts, (part + 1) * PIXELS // parts)
-            runs = slice(part * RUNS // parts, (part + 1) * RUNS // parts)
+            blocks = blocks_of(u, part)
+            columns = slice(blocks.start * PAIR * BLOCK, blocks.stop * PAIR * BLOCK)
+            runs = slice(blocks.start * BLOCK_RUNS, blocks.stop * BLOCK_RUNS)
             nc.vector.quantize_mx(
                 out=x_codes[u][:, cp, columns].bitcast(FP8X4),
                 scales=x_scales[u][:, cp, columns],
                 in_=grouped_tiles[(u, cp)][:, runs].rearrange("p c j i t -> p (c j i t)"),
             )
 
-        def empty_bank(stage, index, out, in_):
-            if stage >= BATCH and index % 2 == 1:
-                nc.vector.tensor_copy(out=out, in_=in_)
-            else:
-                nc.scalar.copy(out=out, in_=in_)
-
         def project(u, part, g):
             tensor = u % 2
-            parts = parts_of(u)
             if part == 0 and g == 0:
-                folded = folded_pool.tile([P, parts, FOLD_PASSES, HALF // parts, PACK], BF16, align_bytes=64)
+                folded = folded_pool.tile([P, FOLD_PASSES * HALF, PACK], BF16, align_bytes=64)
                 folded_tiles[u] = folded
-            folded = folded_tiles[u]
-            for block in range(BLOCKS // parts):
-                first = (part * BLOCKS // parts + block) * PAIR * BLOCK
-                columns = slice(first, first + PAIR * BLOCK)
+            folded = folded_part(folded_tiles[u], u, part).rearrange("m (g n) t -> m g n t", g=FOLD_PASSES)
+            blocks = blocks_of(u, part)
+            for block in range(blocks.start, blocks.stop):
+                columns = slice(block * PAIR * BLOCK, (block + 1) * PAIR * BLOCK)
                 bank = bank_pool.tile([P, PAIR, BLOCK_RUNS, PAIR, RUN], F32, tag="bank")
                 for e in range(PAIR):
                     for cp in range(CHANNEL_PASSES):
@@ -181,80 +195,134 @@ def tile_nonlocalblock_pa_t_kernel(tc, q, k, W_phi, W_theta, out):
                             start=(cp == 0),
                             stop=(cp == CHANNEL_PASSES - 1),
                         )
-                empty_bank(
-                    (u + 1) // 2,
-                    block,
-                    out=folded[:, part, g, block * BLOCK : (block + 1) * BLOCK, :].rearrange(
+                n = (block - blocks.start) * BLOCK
+                nc.scalar.copy(
+                    out=folded[:, g, n : n + BLOCK, :].rearrange(
                         "m (c i) (e j) -> m c i e j", i=RUN, e=PAIR
                     ),
                     in_=bank[:].rearrange("m e c j i -> m c i e j"),
                 )
 
+        def folded_part(tile, u, part):
+            blocks = blocks_of(u, part)
+            return tile[:, blocks.start * FOLD_PASSES * BLOCK : blocks.stop * FOLD_PASSES * BLOCK]
+
         def quantise_fold(u, part):
-            parts = parts_of(u)
             if part == 0:
-                codes = f_pool.tile([P, parts, FOLD_PASSES, HALF // parts], U32, align_bytes=64)
-                scales = f_pool.tile([P, parts, FOLD_PASSES, HALF // parts], U8, align_bytes=64)
+                codes = f_pool.tile([P, FOLD_PASSES * HALF], U32, align_bytes=64)
+                scales = f_pool.tile([P, FOLD_PASSES * HALF], U8, align_bytes=64)
                 f_codes[u] = codes
                 f_scales[u] = scales
             nc.vector.quantize_mx(
-                out=f_codes[u][:, part, :, :].rearrange("m g n -> m (g n)").bitcast(FP8X4),
-                scales=f_scales[u][:, part, :, :].rearrange("m g n -> m (g n)"),
-                in_=folded_tiles[u][:, part, :, :, :].rearrange("m g n t -> m (g n t)"),
+                out=folded_part(f_codes[u], u, part).bitcast(FP8X4),
+                scales=folded_part(f_scales[u], u, part),
+                in_=folded_part(folded_tiles[u], u, part).rearrange("m n t -> m (n t)"),
             )
 
         def affinity(batch, part):
             phi, theta = 2 * batch, 2 * batch + 1
-            parts = parts_of(theta)
-            for tile in range(HALF // P // parts):
+            blocks = blocks_of(theta, part)
+            for block in range(blocks.start, blocks.stop):
                 acc = acc_pool.tile([P, HALF], F32)
+                accs[(batch, block)] = acc
                 for g in range(FOLD_PASSES):
+                    first = ((blocks.stop - blocks.start) * g + block - blocks.start) * BLOCK
+                    rows = slice(first, first + BLOCK)
+                    columns = slice(g * HALF, (g + 1) * HALF)
                     nc.tensor.matmul_mx(
                         out=acc[:],
-                        lhsT=f_codes[theta][:, part, g, tile * P : (tile + 1) * P].bitcast(FP8X4),
-                        lhsT_scale=f_scales[theta][:, part, g, tile * P : (tile + 1) * P],
-                        rhs=f_codes[phi][:, 0, g, :].bitcast(FP8X4),
-                        rhs_scale=f_scales[phi][:, 0, g, :],
+                        lhsT=folded_part(f_codes[theta], theta, part)[:, rows].bitcast(FP8X4),
+                        lhsT_scale=folded_part(f_scales[theta], theta, part)[:, rows],
+                        rhs=f_codes[phi][:, columns].bitcast(FP8X4),
+                        rhs_scale=f_scales[phi][:, columns],
                         start=(g == 0),
                         stop=(g == FOLD_PASSES - 1),
                     )
-                i = part * (HALF // P // parts) + tile
-                result = result_pool.tile([P, HALF], F32)
-                empty_bank(batch + 1, i, out=result[:], in_=acc[:])
-                nc.sync.dma_start(out=out[batch, i * P : (i + 1) * P, :], in_=result[:])
 
-        load_chunk(0, 0)
-        load_weights(0, 0)
-        load_chunk(0, 1)
-        load_weights(0, 1)
-        load_weights(1, 0)
-        load_chunk(1, 0)
-        load_chunk(1, 1)
-        load_weights(1, 1)
-        for u in range(2, LOADS_AHEAD):
+        def empty_accs(batch):
+            for block in range(BLOCKS):
+                acc = accs[(batch, block)]
+                result = result_pool.tile([P, HALF], F32)
+                if batch >= BATCH - 2 and block % 2 == 1:
+                    nc.vector.tensor_copy(out=result[:], in_=acc[:])
+                else:
+                    nc.scalar.copy(out=result[:], in_=acc[:])
+                nc.sync.dma_start(out=out[batch, block * P : (block + 1) * P, :], in_=result[:])
+
+        for u in range(LEAD):
+            for cp in range(CHANNEL_PASSES):
+                load_chunk(u, cp)
+            for g in range(FOLD_PASSES):
+                load_weights(u, g)
+        for u in range(LEAD, LOADS_AHEAD):
             for cp in range(CHANNEL_PASSES):
                 load_chunk(u, cp)
 
-        def prepare(u):
-            for part in range(parts_of(u)):
-                for cp in range(CHANNEL_PASSES):
-                    regroup(u, part, cp)
-                    quantise(u, part, cp)
+        def prepare(u, part):
+            for cp in range(CHANNEL_PASSES):
+                regroup(nc.vector, u, part, cp)
+            for cp in range(CHANNEL_PASSES):
+                quantise(u, part, cp)
 
-        for tensor in range(len(weights)):
+        def product(batch):
+            for part in range(len(parts_of(2 * batch + 1))):
+                affinity(batch, part)
+            empty_accs(batch)
+
+        last = UNITS - 1
+        last_parts = range(len(LAST_PARTS))
+        with tc.manual_schedule(
+            engines={mybir.EngineType.PE, mybir.EngineType.Activation, mybir.EngineType.DVE}
+        ):
+            regroup(nc.vector, 0, 0, 0)
+            quantise(0, 0, 0)
+            regroup(nc.vector, 0, 0, 1)
+            regroup(nc.scalar, 0, 0, 1)
+            transpose_weights(0, 0)
+            quantise(0, 0, 1)
+            transpose_weights(0, 1)
+            quantise_weights(0, 0)
+            quantise_weights(0, 1)
+            project(0, 0, 0)
+            regroup(nc.vector, 1, 0, 0)
+            regroup(nc.vector, 1, 0, 1)
+            regroup(nc.scalar, 1, 0, 1)
+            quantise(1, 0, 0)
+            project(0, 0, 1)
+            quantise(1, 0, 1)
+            transpose_weights(1, 0)
+            transpose_weights(1, 1)
+            quantise_weights(1, 0)
+            quantise_weights(1, 1)
+            for u in range(2, UNITS - 1):
+                if u >= LOADS_AHEAD:
+                    for cp in range(CHANNEL_PASSES):
+                        load_chunk(u, cp)
+                regroup(nc.scalar, u, 0, 1)
+                prepare(u, 0)
+                quantise_fold(u - 2, 0)
+                project(u - 1, 0, 0)
+                if u >= 4 and u % 2 == 0:
+                    product(u // 2 - 2)
+                project(u - 1, 0, 1)
+            for cp in range(CHANNEL_PASSES):
+                load_chunk(last, cp)
+            regroup(nc.scalar, last, 0, 1)
+            prepare(last, 0)
+            quantise_fold(last - 2, 0)
             for g in range(FOLD_PASSES):
-                pack_weights(tensor, g)
-        for u in range(LEAD):
-            prepare(u)
-        for u in range(UNITS):
-            if u + LOADS_AHEAD < UNITS:
-                for cp in range(CHANNEL_PASSES):
-                    load_chunk(u + LOADS_AHEAD, cp)
-            if u + LEAD < UNITS:
-                prepare(u + LEAD)
-            for part in range(parts_of(u)):
+                project(last - 1, 0, g)
+            for part in last_parts[1:]:
+                regroup(nc.scalar, last, part, 1)
+                prepare(last, part)
+            quantise_fold(last - 1, 0)
+            for g in range(FOLD_PASSES):
+                project(last, 0, g)
+            product(BATCH - 2)
+            quantise_fold(last, 0)
+            for part in last_parts[1:]:
                 for g in range(FOLD_PASSES):
-                    project(u, part, g)
-                quantise_fold(u, part)
-                if u % 2 == 1:
-                    affinity(u // 2, part)
+                    project(last, part, g)
+            for part in last_parts[1:]:
+                quantise_fold(last, part)
+            product(BATCH - 1)

@@ -138,6 +138,9 @@ def tile_nonlocalblock_pa_t_kernel(tc, q, k, W_phi, W_theta, out):
             first = sum(parts_of(u)[:part])
             return slice(first, first + parts_of(u)[part])
 
+        def part_of(u, block):
+            return [p for p in range(len(parts_of(u))) if blocks_of(u, p).start <= block < blocks_of(u, p).stop][0]
+
         def regroup(engine, u, part, cp):
             if (u, cp) not in grouped_tiles:
                 grouped = grouped_pool.tile([P, RUNS, PAIR, RUN, PACK], BF16, align_bytes=64)
@@ -219,14 +222,15 @@ def tile_nonlocalblock_pa_t_kernel(tc, q, k, W_phi, W_theta, out):
                 in_=folded_part(folded_tiles[u], u, part).rearrange("m n t -> m (n t)"),
             )
 
-        def affinity(batch, part):
+        def affinity(batch, blocks):
             phi, theta = 2 * batch, 2 * batch + 1
-            blocks = blocks_of(theta, part)
-            for block in range(blocks.start, blocks.stop):
+            for block in blocks:
+                part = part_of(theta, block)
+                own = blocks_of(theta, part)
                 acc = acc_pool.tile([P, HALF], F32)
                 accs[(batch, block)] = acc
                 for g in range(FOLD_PASSES):
-                    first = ((blocks.stop - blocks.start) * g + block - blocks.start) * BLOCK
+                    first = ((own.stop - own.start) * g + block - own.start) * BLOCK
                     rows = slice(first, first + BLOCK)
                     columns = slice(g * HALF, (g + 1) * HALF)
                     nc.tensor.matmul_mx(
@@ -239,8 +243,8 @@ def tile_nonlocalblock_pa_t_kernel(tc, q, k, W_phi, W_theta, out):
                         stop=(g == FOLD_PASSES - 1),
                     )
 
-        def empty_accs(batch):
-            for block in range(BLOCKS):
+        def empty_accs(batch, blocks):
+            for block in blocks:
                 acc = accs[(batch, block)]
                 result = result_pool.tile([P, HALF], F32)
                 if batch >= BATCH - 2 and block % 2 == 1:
@@ -259,15 +263,22 @@ def tile_nonlocalblock_pa_t_kernel(tc, q, k, W_phi, W_theta, out):
                 load_chunk(u, cp)
 
         def prepare(u, part):
-            for cp in range(CHANNEL_PASSES):
-                regroup(nc.vector, u, part, cp)
+            regroup(nc.vector, u, part, 0)
+            if u == 2:
+                for g in range(FOLD_PASSES):
+                    quantise_weights(1, g)
+            regroup(nc.vector, u, part, 1)
             for cp in range(CHANNEL_PASSES):
                 quantise(u, part, cp)
 
-        def product(batch):
-            for part in range(len(parts_of(2 * batch + 1))):
-                affinity(batch, part)
-            empty_accs(batch)
+        def product(batch, blocks):
+            affinity(batch, blocks)
+            empty_accs(batch, blocks)
+
+        def half_product(u):
+            if u >= 4:
+                half = u % 2 * (BLOCKS // 2)
+                product(u // 2 - 2, range(half, half + BLOCKS // 2))
 
         last = UNITS - 1
         last_parts = range(len(LAST_PARTS))
@@ -292,8 +303,6 @@ def tile_nonlocalblock_pa_t_kernel(tc, q, k, W_phi, W_theta, out):
             quantise(1, 0, 1)
             transpose_weights(1, 0)
             transpose_weights(1, 1)
-            quantise_weights(1, 0)
-            quantise_weights(1, 1)
             for u in range(2, UNITS - 1):
                 if u >= LOADS_AHEAD:
                     for cp in range(CHANNEL_PASSES):
@@ -302,27 +311,27 @@ def tile_nonlocalblock_pa_t_kernel(tc, q, k, W_phi, W_theta, out):
                 prepare(u, 0)
                 quantise_fold(u - 2, 0)
                 project(u - 1, 0, 0)
-                if u >= 4 and u % 2 == 0:
-                    product(u // 2 - 2)
+                half_product(u)
                 project(u - 1, 0, 1)
             for cp in range(CHANNEL_PASSES):
                 load_chunk(last, cp)
             regroup(nc.scalar, last, 0, 1)
             prepare(last, 0)
             quantise_fold(last - 2, 0)
-            for g in range(FOLD_PASSES):
-                project(last - 1, 0, g)
+            project(last - 1, 0, 0)
+            half_product(last)
+            project(last - 1, 0, 1)
             for part in last_parts[1:]:
                 regroup(nc.scalar, last, part, 1)
                 prepare(last, part)
             quantise_fold(last - 1, 0)
             for g in range(FOLD_PASSES):
                 project(last, 0, g)
-            product(BATCH - 2)
+            product(BATCH - 2, range(BLOCKS))
             quantise_fold(last, 0)
             for part in last_parts[1:]:
                 for g in range(FOLD_PASSES):
                     project(last, part, g)
             for part in last_parts[1:]:
                 quantise_fold(last, part)
-            product(BATCH - 1)
+            product(BATCH - 1, range(BLOCKS))

@@ -118,6 +118,12 @@ def tile_nonlocalblock_pa_t_kernel(tc, q, k, W_phi, W_theta, out):
                 in_=w_grouped[:].rearrange("p cp x t -> p (cp x t)"),
             )
 
+        def warm_up(count):
+            pixels = raw_halves[0][:, 0, :]
+            bank = bank_pool.tile([P, HALF], F32, name="warm", tag="bank")
+            for repeat in range(count):
+                nc.tensor.matmul(out=bank[:], lhsT=pixels[:, :P], rhs=pixels, start=True, stop=True)
+
         def load_chunk(u, cp):
             batch, tensor = divmod(u, 2)
             rows = maps[tensor][batch, cp * K_PASS : (cp + 1) * K_PASS, :].rearrange("(p t) w -> p t w", t=PACK)
@@ -289,9 +295,12 @@ def tile_nonlocalblock_pa_t_kernel(tc, q, k, W_phi, W_theta, out):
             quantise(0, 0, 0)
             regroup(nc.vector, 0, 0, 1)
             regroup(nc.scalar, 0, 0, 1)
+            warm_up(8)
             transpose_weights(0, 0)
+            warm_up(2)
             quantise(0, 0, 1)
             transpose_weights(0, 1)
+            warm_up(2)
             quantise_weights(0, 0)
             quantise_weights(0, 1)
             project(0, 0, 0)
@@ -303,6 +312,7 @@ def tile_nonlocalblock_pa_t_kernel(tc, q, k, W_phi, W_theta, out):
             quantise(1, 0, 1)
             transpose_weights(1, 0)
             transpose_weights(1, 1)
+            warm_up(3)
             for u in range(2, UNITS - 1):
                 if u >= LOADS_AHEAD:
                     for cp in range(CHANNEL_PASSES):

@@ -118,9 +118,9 @@ def tile_nonlocalblock_pa_t_kernel(tc, q, k, W_phi, W_theta, out):
                 in_=w_grouped[:].rearrange("p cp x t -> p (cp x t)"),
             )
 
-        def warm_up(count):
+        def warm_up(count, pool, tag):
             pixels = raw_halves[0][:, 0, :]
-            bank = bank_pool.tile([P, HALF], F32, name="warm", tag="bank")
+            bank = pool.tile([P, HALF], F32, name="warm", tag=tag)
             for repeat in range(count):
                 nc.tensor.matmul(out=bank[:], lhsT=pixels[:, :P], rhs=pixels, start=True, stop=True)
 
@@ -233,7 +233,7 @@ def tile_nonlocalblock_pa_t_kernel(tc, q, k, W_phi, W_theta, out):
             for block in blocks:
                 part = part_of(theta, block)
                 own = blocks_of(theta, part)
-                acc = acc_pool.tile([P, HALF], F32)
+                acc = acc_pool.tile([P, HALF], F32, tag="acc")
                 accs[(batch, block)] = acc
                 for g in range(FOLD_PASSES):
                     first = ((own.stop - own.start) * g + block - own.start) * BLOCK
@@ -295,12 +295,12 @@ def tile_nonlocalblock_pa_t_kernel(tc, q, k, W_phi, W_theta, out):
             quantise(0, 0, 0)
             regroup(nc.vector, 0, 0, 1)
             regroup(nc.scalar, 0, 0, 1)
-            warm_up(8)
+            warm_up(8, bank_pool, "bank")
             transpose_weights(0, 0)
-            warm_up(2)
+            warm_up(2, bank_pool, "bank")
             quantise(0, 0, 1)
             transpose_weights(0, 1)
-            warm_up(2)
+            warm_up(2, bank_pool, "bank")
             quantise_weights(0, 0)
             quantise_weights(0, 1)
             project(0, 0, 0)
@@ -312,7 +312,7 @@ def tile_nonlocalblock_pa_t_kernel(tc, q, k, W_phi, W_theta, out):
             quantise(1, 0, 1)
             transpose_weights(1, 0)
             transpose_weights(1, 1)
-            warm_up(3)
+            warm_up(3, bank_pool, "bank")
             for u in range(2, UNITS - 1):
                 if u >= LOADS_AHEAD:
                     for cp in range(CHANNEL_PASSES):
@@ -323,6 +323,7 @@ def tile_nonlocalblock_pa_t_kernel(tc, q, k, W_phi, W_theta, out):
                 project(u - 1, 0, 0)
                 half_product(u)
                 project(u - 1, 0, 1)
+                warm_up(2, acc_pool, "acc")
             for cp in range(CHANNEL_PASSES):
                 load_chunk(last, cp)
             regroup(nc.scalar, last, 0, 1)

from contextlib import ExitStack

import concourse.mybir as mybir
from concourse.masks import make_identity

BF16 = mybir.dt.bfloat16
F32 = mybir.dt.float32
U32 = mybir.dt.uint32
U8 = mybir.dt.uint8
FP8X4 = mybir.dt.float8_e4m3fn_x4

BATCH = 4
CHANNELS = 1024
PIXELS = 1024
INTER = 512
HALF = PIXELS // 2

P = 128
PACK = 4
K_PASS = P * PACK
CHANNEL_PASSES = CHANNELS // K_PASS
FOLD_PASSES = 2 * INTER // K_PASS
PAIR = 2
BLOCK = 128
BLOCKS = HALF // BLOCK
RUN = 8
RUNS = HALF // RUN
BLOCK_RUNS = BLOCK // RUN
SCALAR_RUNS = 6

UNITS = 2 * BATCH
LAST_PARTS = (2, 1, 1)
LEAD = 2
LOADS_AHEAD = 4

FLOPS = 2 * BATCH * (2 * INTER * CHANNELS * PIXELS + HALF * HALF * 2 * INTER)


def tile_nonlocalblock_pa_t_kernel(tc, q, k, W_phi, W_theta, out):
    nc = tc.nc
    maps = (q.rearrange("b c h w -> b c (h w)"), k.rearrange("b c h w -> b c (h w)"))
    weights = (W_phi, W_theta)

    with ExitStack() as ctx:
        const_pool = ctx.enter_context(tc.tile_pool(name="const", bufs=1))
        w_rows_pool = ctx.enter_context(tc.tile_pool(name="w_rows", bufs=2 * FOLD_PASSES))
        w_grouped_pool = ctx.enter_context(tc.tile_pool(name="w_grouped", bufs=2))
        raw_pool = ctx.enter_context(tc.tile_pool(name="raw", bufs=LOADS_AHEAD * CHANNEL_PASSES))
        grouped_pool = ctx.enter_context(tc.tile_pool(name="grouped", bufs=4))
        x_pool = ctx.enter_context(tc.tile_pool(name="x", bufs=LEAD + 2))
        folded_pool = ctx.enter_context(tc.tile_pool(name="folded", bufs=3))
        f_pool = ctx.enter_context(tc.tile_pool(name="f", bufs=4))
        result_pool = ctx.enter_context(tc.tile_pool(name="result", bufs=6))
        bank_pool = ctx.enter_context(tc.psum_pool(name="bank", bufs=4))
        acc_pool = ctx.enter_context(tc.psum_pool(name="acc", bufs=HALF // P))

        identity = const_pool.tile([P, P], F32)
        make_identity(nc, identity[:])

        w_codes = []
        w_scales = []
        for tensor in range(len(weights)):
            codes = const_pool.tile(
                [P, FOLD_PASSES, CHANNEL_PASSES, PAIR, P], U32, name="w_codes_%d" % tensor, align_bytes=64
            )
            scales = const_pool.tile(
                [P, FOLD_PASSES, CHANNEL_PASSES, PAIR, P], U8, name="w_scales_%d" % tensor, align_bytes=64
            )
            w_codes.append(codes)
            w_scales.append(scales)

        w_rows_tiles = {}
        w_grouped_tiles = {}
        raw_tiles = {}
        raw_halves = []
        grouped_tiles = {}
        x_codes = {}
        x_scales = {}
        folded_tiles = {}
        f_codes = {}
        f_scales = {}
        accs = {}

        def load_weights(tensor, g):
            w_rows = w_rows_pool.tile([P, PAIR, CHANNELS], BF16)
            rows = weights[tensor][g * PAIR * P : (g + 1) * PAIR * P, :]
            nc.sync.dma_start(out=w_rows[:], in_=rows.rearrange("(m e) c -> m e c", e=PAIR))
            w_rows_tiles[(tensor, g)] = w_rows

        def transpose_weights(tensor, g):
            w_rows = w_rows_tiles[(tensor, g)]
            words = (
                w_rows[:]
                .rearrange("m e c -> m (e c)")
                .bitcast(F32)
                .rearrange("m (e cp p u) -> m e cp p u", e=PAIR, cp=CHANNEL_PASSES, u=2)
            )
            w_grouped = w_grouped_pool.tile([P, CHANNEL_PASSES, PAIR * P, PACK], BF16, align_bytes=64)
            for cp in range(CHANNEL_PASSES):
                flipped = bank_pool.tile([P, 2, PAIR, P], F32, tag="bank")
                for u in range(2):
                    for e in range(PAIR):
                        nc.tensor.transpose(flipped[:, u, e, :], words[:, e, cp, :, u], identity[:])
                nc.scalar.copy(
                    out=w_grouped[:, cp, :, :]
                    .rearrange("p x t -> p (x t)")
                    .bitcast(F32)
                    .rearrange("p (x u) -> p x u", u=2),
                    in_=flipped[:].rearrange("p u e m -> p (e m) u"),
                )
            w_grouped_tiles[(tensor, g)] = w_grouped

        def quantise_weights(tensor, g):
            w_grouped = w_grouped_tiles[(tensor, g)]
            nc.vector.quantize_mx(
                out=w_codes[tensor][:, g, :, :, :].rearrange("p cp e m -> p (cp e m)").bitcast(FP8X4),
                scales=w_scales[tensor][:, g, :, :, :].rearrange("p cp e m -> p (cp e m)"),
                in_=w_grouped[:].rearrange("p cp x t -> p (cp x t)"),
            )

        def warm_up(count, pool, tag):
            pixels = raw_halves[0][:, 0, :]
            bank = pool.tile([P, HALF], F32, name="warm", tag=tag)
            for repeat in range(count):
                nc.tensor.matmul(out=bank[:], lhsT=pixels[:, :P], rhs=pixels, start=True, stop=True)

        def load_chunk(u, cp):
            batch, tensor = divmod(u, 2)
            rows = maps[tensor][batch, cp * K_PASS : (cp + 1) * K_PASS, :].rearrange("(p t) w -> p t w", t=PACK)
            if u == 0 and cp == 0:
                for j in range(PAIR):
                    raw_half = const_pool.tile([P, PACK, HALF], BF16, name="raw_half_%d" % j)
                    nc.sync.dma_start(out=raw_half[:], in_=rows[:, :, j * HALF : (j + 1) * HALF])
                    raw_halves.append(raw_half)
            else:
                raw = raw_pool.tile([P, PACK, PIXELS], BF16)
                nc.sync.dma_start(out=raw[:], in_=rows)
                raw_tiles[(u, cp)] = raw

        def parts_of(u):
            return LAST_PARTS if u == UNITS - 1 else (BLOCKS,)

        def blocks_of(u, part):
            first = sum(parts_of(u)[:part])
            return slice(first, first + parts_of(u)[part])

        def part_of(u, block):
            return [p for p in range(len(parts_of(u))) if blocks_of(u, p).start <= block < blocks_of(u, p).stop][0]

        def regroup(engine, u, part, cp):
            if (u, cp) not in grouped_tiles:
                grouped = grouped_pool.tile([P, RUNS, PAIR, RUN, PACK], BF16, align_bytes=64)
                grouped_tiles[(u, cp)] = grouped
            grouped = grouped_tiles[(u, cp)]
            target = grouped[:].rearrange("p c j i t -> p c j t i")
            if u == 0 and cp == 0:
                for j in range(PAIR):
                    nc.vector.tensor_copy(
                        out=target[:, :, j], in_=raw_halves[j][:].rearrange("p t (c i) -> p c t i", i=RUN)
                    )
                return
            source = raw_tiles[(u, cp)][:].rearrange("p t (j c i) -> p c j t i", j=PAIR, i=RUN)
            blocks = blocks_of(u, part)
            begin, end = blocks.start * BLOCK_RUNS, blocks.stop * BLOCK_RUNS
            middle = end - (blocks.stop - blocks.start) * SCALAR_RUNS if cp == CHANNEL_PASSES - 1 else end
            if engine is nc.scalar:
                nc.scalar.copy(out=target[:, middle:end], in_=source[:, middle:end])
            else:
                nc.vector.tensor_copy(out=target[:, begin:middle], in_=source[:, begin:middle])

        def quantise(u, part, cp):
            if part == 0 and cp == 0:
                codes = x_pool.tile([P, CHANNEL_PASSES, PIXELS], U32, align_bytes=64)
                scales = x_pool.tile([P, CHANNEL_PASSES, PIXELS], U8, align_bytes=64)
                x_codes[u] = codes
                x_scales[u] = scales
            blocks = blocks_of(u, part)
            columns = slice(blocks.start * PAIR * BLOCK, blocks.stop * PAIR * BLOCK)
            runs = slice(blocks.start * BLOCK_RUNS, blocks.stop * BLOCK_RUNS)
            nc.vector.quantize_mx(
                out=x_codes[u][:, cp, columns].bitcast(FP8X4),
                scales=x_scales[u][:, cp, columns],
                in_=grouped_tiles[(u, cp)][:, runs].rearrange("p c j i t -> p (c j i t)"),
            )

        def project(u, part, g):
            tensor = u % 2
            if part == 0 and g == 0:
                folded = folded_pool.tile([P, FOLD_PASSES * HALF, PACK], BF16, align_bytes=64)
                folded_tiles[u] = folded
            folded = folded_part(folded_tiles[u], u, part).rearrange("m (g n) t -> m g n t", g=FOLD_PASSES)
            blocks = blocks_of(u, part)
            for block in range(blocks.start, blocks.stop):
                columns = slice(block * PAIR * BLOCK, (block + 1) * PAIR * BLOCK)
                bank = bank_pool.tile([P, PAIR, BLOCK_RUNS, PAIR, RUN], F32, tag="bank")
                for e in range(PAIR):
                    for cp in range(CHANNEL_PASSES):
                        nc.tensor.matmul_mx(
                            out=bank[:, e, :, :, :].rearrange("m c j i -> m (c j i)"),
                            lhsT=w_codes[tensor][:, g, cp, e, :].bitcast(FP8X4),
                            lhsT_scale=w_scales[tensor][:, g, cp, e, :],
                            rhs=x_codes[u][:, cp, columns].bitcast(FP8X4),
                            rhs_scale=x_scales[u][:, cp, columns],
                            start=(cp == 0),
                            stop=(cp == CHANNEL_PASSES - 1),
                        )
                n = (block - blocks.start) * BLOCK
                nc.scalar.copy(
                    out=folded[:, g, n : n + BLOCK, :].rearrange(
                        "m (c i) (e j) -> m c i e j", i=RUN, e=PAIR
                    ),
                    in_=bank[:].rearrange("m e c j i -> m c i e j"),
                )

        def folded_part(tile, u, part):
            blocks = blocks_of(u, part)
            return tile[:, blocks.start * FOLD_PASSES * BLOCK : blocks.stop * FOLD_PASSES * BLOCK]

        def quantise_fold(u, part):
            if part == 0:
                codes = f_pool.tile([P, FOLD_PASSES * HALF], U32, align_bytes=64)
                scales = f_pool.tile([P, FOLD_PASSES * HALF], U8, align_bytes=64)
                f_codes[u] = codes
                f_scales[u] = scales
            nc.vector.quantize_mx(
                out=folded_part(f_codes[u], u, part).bitcast(FP8X4),
                scales=folded_part(f_scales[u], u, part),
                in_=folded_part(folded_tiles[u], u, part).rearrange("m n t -> m (n t)"),
            )

        def affinity(batch, blocks):
            phi, theta = 2 * batch, 2 * batch + 1
            for block in blocks:
                part = part_of(theta, block)
                own = blocks_of(theta, part)
                acc = acc_pool.tile([P, HALF], F32, tag="acc")
                accs[(batch, block)] = acc
                for g in range(FOLD_PASSES):
                    first = ((own.stop - own.start) * g + block - own.start) * BLOCK
                    rows = slice(first, first + BLOCK)
                    columns = slice(g * HALF, (g + 1) * HALF)
                    nc.tensor.matmul_mx(
                        out=acc[:],
                        lhsT=folded_part(f_codes[theta], theta, part)[:, rows].bitcast(FP8X4),
                        lhsT_scale=folded_part(f_scales[theta], theta, part)[:, rows],
                        rhs=f_codes[phi][:, columns].bitcast(FP8X4),
                        rhs_scale=f_scales[phi][:, columns],
                        start=(g == 0),
                        stop=(g == FOLD_PASSES - 1),
                    )

        def empty_accs(batch, blocks):
            for block in blocks:
                acc = accs[(batch, block)]
                result = result_pool.tile([P, HALF], F32)
                if batch >= BATCH - 2 and block % 2 == 1:
                    nc.vector.tensor_copy(out=result[:], in_=acc[:])
                else:
                    nc.scalar.copy(out=result[:], in_=acc[:])
                nc.sync.dma_start(out=out[batch, block * P : (block + 1) * P, :], in_=result[:])

        for u in range(LEAD):
            for cp in range(CHANNEL_PASSES):
                load_chunk(u, cp)
            for g in range(FOLD_PASSES):
                load_weights(u, g)
        for u in range(LEAD, LOADS_AHEAD):
            for cp in range(CHANNEL_PASSES):
                load_chunk(u, cp)

        def prepare(u, part):
            regroup(nc.vector, u, part, 0)
            if u == 2:
                for g in range(FOLD_PASSES):
                    quantise_weights(1, g)
            regroup(nc.vector, u, part, 1)
            for cp in range(CHANNEL_PASSES):
                quantise(u, part, cp)

        def product(batch, blocks):
            affinity(batch, blocks)
            empty_accs(batch, blocks)

        def half_product(u):
            if u >= 4:
                half = u % 2 * (BLOCKS // 2)
                product(u // 2 - 2, range(half, half + BLOCKS // 2))

        last = UNITS - 1
        last_parts = range(len(LAST_PARTS))
        with tc.manual_schedule(
            engines={mybir.EngineType.PE, mybir.EngineType.Activation, mybir.EngineType.DVE}
        ):
            regroup(nc.vector, 0, 0, 0)
            quantise(0, 0, 0)
            regroup(nc.vector, 0, 0, 1)
            regroup(nc.scalar, 0, 0, 1)
            warm_up(8, bank_pool, "bank")
            transpose_weights(0, 0)
            warm_up(2, bank_pool, "bank")
            quantise(0, 0, 1)
            transpose_weights(0, 1)
            warm_up(2, bank_pool, "bank")
            quantise_weights(0, 0)
            quantise_weights(0, 1)
            project(0, 0, 0)
            regroup(nc.vector, 1, 0, 0)
            regroup(nc.vector, 1, 0, 1)
            regroup(nc.scalar, 1, 0, 1)
            quantise(1, 0, 0)
            project(0, 0, 1)
            quantise(1, 0, 1)
            transpose_weights(1, 0)
            transpose_weights(1, 1)
            warm_up(3, bank_pool, "bank")
            for u in range(2, UNITS - 1):
                if u >= LOADS_AHEAD:
                    for cp in range(CHANNEL_PASSES):
                        load_chunk(u, cp)
                regroup(nc.scalar, u, 0, 1)
                prepare(u, 0)
                quantise_fold(u - 2, 0)
                project(u - 1, 0, 0)
                half_product(u)
                project(u - 1, 0, 1)
                warm_up(2, acc_pool, "acc")
            for cp in range(CHANNEL_PASSES):
                load_chunk(last, cp)
            regroup(nc.scalar, last, 0, 1)
            prepare(last, 0)
            quantise_fold(last - 2, 0)
            project(last - 1, 0, 0)
            half_product(last)
            project(last - 1, 0, 1)
            for part in last_parts[1:]:
                regroup(nc.scalar, last, part, 1)
                prepare(last, part)
            quantise_fold(last - 1, 0)
            for g in range(FOLD_PASSES):
                project(last, 0, g)
            product(BATCH - 2, range(BLOCKS))
            quantise_fold(last, 0)
            for part in last_parts[1:]:
                for g in range(FOLD_PASSES):
                    project(last, part, g)
            for part in last_parts[1:]:
                quantise_fold(last, part)
            product(BATCH - 1, range(BLOCKS))
